import numpy as np
import ml_dtypes

BF16 = ml_dtypes.bfloat16


def bf(x):
    return np.asarray(x, np.float32).astype(BF16)


def f32(x):
    return np.asarray(x, np.float32)


def f64(x):
    return np.asarray(x).astype(np.float64)


def striped(idx):
    return np.tile(idx.reshape(-1, 16).T, (8, 1))


HK, D, C, S, N, M = 4, 128, 512, 4096, 2048, 1024
SCALE = 1.0 / np.sqrt(D)


def setup_inputs():
    kt = f32(np.random.standard_normal((C, S)))
    ksc = f32(np.repeat(0.5 + np.random.uniform(size=(HK, N)), D, axis=0))
    q = bf(1.5 * np.random.standard_normal((C, M)))
    v = f32(2.0 * np.random.standard_normal((N, C)))
    vsc = f32(0.5 + np.random.uniform(size=(N, HK)))
    return {"kt": kt, "ksc": ksc, "q": q, "v": v, "vsc": vsc, "offs": striped(np.random.permutation(S)[:N])}


def reference(kt, ksc, q, v, vsc, offs):
    idx = offs[:16].T.reshape(-1)
    kd = f64(kt)[:, idx] * f64(ksc)
    vd = f64(v).reshape(N, HK, D) * f64(vsc)[:, :, None]
    qq = f64(q)
    res = np.empty((C, M), np.float64)
    for h in range(HK):
        r = slice(h * D, (h + 1) * D)
        s = SCALE * (kd[r].T @ qq[r])
        e = np.exp(s)
        p = e / e.sum(axis=0, keepdims=True)
        res[r] = vd[:, h, :].T @ p
    return res

@@ -1,0 +1,132 @@
+import math
+
+import concourse.mybir as mybir
+from concourse.masks import make_identity
+
+F32 = mybir.dt.float32
+BF16 = mybir.dt.bfloat16
+U16 = mybir.dt.uint16
+MULT = mybir.AluOpType.mult
+EXP = mybir.ActivationFunctionType.Exp
+
+P = 128
+HEADS = 4
+D = 128
+S = 4096
+N = 2048
+M = 1024
+SCALE = 1.0 / math.sqrt(D)
+
+PIECE = 512
+PIECES = N // PIECE
+BLOCKS = N // P
+QUERIES = 256
+UNITS = M // QUERIES
+PAIRS = BLOCKS // 2
+VD_STEP = D + 16
+
+FLOPS = 2 * 2 * HEADS * D * N * M
+
+
+def tile_sfaanetwork_b_kernel(tc, kt, ksc, q, v, vsc, offs, out):
+    nc = tc.nc
+    with (
+        tc.tile_pool(name="held", bufs=1) as held,
+        tc.tile_pool(name="products", bufs=3) as products,
+        tc.tile_pool(name="weights", bufs=6) as weights,
+        tc.tile_pool(name="results", bufs=4) as results,
+        tc.psum_pool(name="score_banks", bufs=3) as score_banks,
+        tc.psum_pool(name="sum_banks", bufs=4) as sum_banks,
+        tc.psum_pool(name="flip_banks", bufs=1) as flip_banks,
+    ):
+        offsets = held.tile([P, N // 16], U16, name="offsets")
+        nc.sync.dma_start(offsets[:], offs)
+        vsc_sb = held.tile([P, BLOCKS, HEADS], F32, name="vsc_sb")
+        v_blocks = v.rearrange("(b p) c -> p b c", p=P)
+        kt_sb, ksc_sb, q_sb, v_sb = [], [], [], []
+        for h in range(HEADS):
+            rows = slice(h * D, (h + 1) * D)
+            kt_sb.append(held.tile([P, S], F32, name=f"kt{h}"))
+            ksc_sb.append(held.tile([P, N], F32, name=f"ksc{h}"))
+            q_sb.append(held.tile([P, M], BF16, name=f"q{h}"))
+            v_sb.append(held.tile([P, BLOCKS, D], F32, name=f"v{h}"))
+            nc.sync.dma_start(kt_sb[h][:], kt[rows, :])
+            nc.sync.dma_start(ksc_sb[h][:], ksc[rows, :])
+            nc.sync.dma_start(q_sb[h][:], q[rows, :])
+            if h == 0:
+                nc.sync.dma_start(vsc_sb[:], vsc.rearrange("(b p) h -> p b h", p=P))
+            nc.sync.dma_start(v_sb[h][:], v_blocks[:, :, rows])
+
+        identity = held.tile([P, P], F32, name="identity")
+        make_identity(nc, identity[:])
+
+        kd_bf = [held.tile([P, N], BF16, name=f"kd_bf{h}") for h in range(HEADS)]
+        vd_one = [held.tile([P, BLOCKS, VD_STEP], BF16, name=f"vd_one{h}") for h in range(HEADS)]
+
+        def dequantise_keys(h, piece):
+            cols = slice(piece * PIECE, (piece + 1) * PIECE)
+            kd = products.tile([P, PIECE], F32, name="kd")
+            nc.vector.tensor_tensor(
+                kd[:],
+                kt_sb[h][:].indirect(offsets[:, piece * (PIECE // 16) : (piece + 1) * (PIECE // 16)]),
+                ksc_sb[h][:, cols],
+                MULT,
+            )
+            nc.vector.tensor_copy(kd_bf[h][:, cols], kd[:])
+
+        def dequantise_values(h):
+            nc.gpsimd.memset(vd_one[h][:, :, D : D + 1], 1.0)
+            nc.gpsimd.tensor_tensor(
+                vd_one[h][:, :, 0:D],
+                v_sb[h][:],
+                vsc_sb[:, :, h : h + 1].to_broadcast([P, BLOCKS, D]),
+                MULT,
+            )
+
+        def attend(h, unit):
+            first = unit * QUERIES
+            sums = [sum_banks.tile([P, D + 1], F32, name="sums") for i in range(QUERIES // P)]
+            for pair in range(PAIRS):
+                scores = score_banks.tile([P, 2, QUERIES], F32, name="scores")
+                for k in range(2):
+                    block = 2 * pair + k
+                    nc.tensor.matmul(
+                        scores[:, k, :],
+                        lhsT=kd_bf[h][:, block * P : (block + 1) * P],
+                        rhs=q_sb[h][:, first : first + QUERIES],
+                        start=True,
+                        stop=True,
+                    )
+                e = weights.tile([P, 2, QUERIES], BF16, name="e")
+                nc.scalar.activation(out=e[:], in_=scores[:], func=EXP, scale=SCALE)
+                for k in range(2):
+                    block = 2 * pair + k
+                    for i in range(QUERIES // P):
+                        nc.tensor.matmul(
+                            sums[i][:],
+                            lhsT=e[:, k, i * P : (i + 1) * P],
+                            rhs=vd_one[h][:, block, 0 : D + 1],
+                            start=(block == 0),
+                            stop=(block == BLOCKS - 1),
+                        )
+            flipped = flip_banks.tile([P, QUERIES], F32, name="flipped")
+            for i in range(QUERIES // P):
+                inverse = results.tile([P, 1], F32, name="inverse")
+                nc.vector.reciprocal(inverse[:], sums[i][:, D : D + 1])
+                normal = results.tile([P, D], F32, name="normal")
+                nc.vector.tensor_scalar_mul(normal[:], sums[i][:, 0:D], inverse[:])
+                nc.tensor.transpose(flipped[:, i * P : (i + 1) * P], normal[:], identity[:])
+            answer = results.tile([P, QUERIES], F32, name="answer")
+            nc.vector.tensor_copy(answer[:], flipped[:])
+            nc.sync.dma_start(out[h * D : (h + 1) * D, first : first + QUERIES], answer[:])
+
+        for piece in range(PIECES):
+            dequantise_keys(0, piece)
+        dequantise_values(0)
+        for h in range(HEADS):
+            for unit in range(UNITS):
+                if h + 1 < HEADS:
+                    dequantise_keys(h + 1, unit)
+                    if unit == 0:
+                        dequantise_values(h + 1)
+                attend(h, unit)

@@ -23,6 +23,7 @@ BLOCKS = N // P
 QUERIES = 256
 UNITS = M // QUERIES
 PAIRS = BLOCKS // 2
+AHEAD = 2
 VD_STEP = D + 16
 
 FLOPS = 2 * 2 * HEADS * D * N * M
@@ -83,32 +84,36 @@ def tile_sfaanetwork_b_kernel(tc, kt, ksc, q, v, vsc, offs, out):
                 MULT,
             )
 
-        def attend(h, unit):
+        def score(h, unit, pair):
             first = unit * QUERIES
-            sums = [sum_banks.tile([P, D + 1], F32, name="sums") for i in range(QUERIES // P)]
-            for pair in range(PAIRS):
-                scores = score_banks.tile([P, 2, QUERIES], F32, name="scores")
-                for k in range(2):
-                    block = 2 * pair + k
+            scores = score_banks.tile([P, 2, QUERIES], F32, name="scores")
+            for k in range(2):
+                block = 2 * pair + k
+                nc.tensor.matmul(
+                    scores[:, k, :],
+                    lhsT=kd_bf[h][:, block * P : (block + 1) * P],
+                    rhs=q_sb[h][:, first : first + QUERIES],
+                    start=True,
+                    stop=True,
+                )
+            return scores
+
+        def weigh(h, pair, scores, sums):
+            e = weights.tile([P, 2, QUERIES], BF16, name="e")
+            nc.scalar.activation(out=e[:], in_=scores[:], func=EXP, scale=SCALE)
+            for k in range(2):
+                block = 2 * pair + k
+                for i in range(QUERIES // P):
                     nc.tensor.matmul(
-                        scores[:, k, :],
-                        lhsT=kd_bf[h][:, block * P : (block + 1) * P],
-                        rhs=q_sb[h][:, first : first + QUERIES],
-                        start=True,
-                        stop=True,
+                        sums[i][:],
+                        lhsT=e[:, k, i * P : (i + 1) * P],
+                        rhs=vd_one[h][:, block, 0 : D + 1],
+                        start=(block == 0),
+                        stop=(block == BLOCKS - 1),
                     )
-                e = weights.tile([P, 2, QUERIES], BF16, name="e")
-                nc.scalar.activation(out=e[:], in_=scores[:], func=EXP, scale=SCALE)
-                for k in range(2):
-                    block = 2 * pair + k
-                    for i in range(QUERIES // P):
-                        nc.tensor.matmul(
-                            sums[i][:],
-                            lhsT=e[:, k, i * P : (i + 1) * P],
-                            rhs=vd_one[h][:, block, 0 : D + 1],
-                            start=(block == 0),
-                            stop=(block == BLOCKS - 1),
-                        )
+
+        def finish(h, unit, sums):
+            first = unit * QUERIES
             flipped = flip_banks.tile([P, QUERIES], F32, name="flipped")
             for i in range(QUERIES // P):
                 inverse = results.tile([P, 1], F32, name="inverse")
@@ -123,10 +128,22 @@ def tile_sfaanetwork_b_kernel(tc, kt, ksc, q, v, vsc, offs, out):
         for piece in range(PIECES):
             dequantise_keys(0, piece)
         dequantise_values(0)
-        for h in range(HEADS):
-            for unit in range(UNITS):
-                if h + 1 < HEADS:
+
+        steps = [(h, unit, pair) for h in range(HEADS) for unit in range(UNITS) for pair in range(PAIRS)]
+        banks = []
+        sums = []
+        for t in range(len(steps) + AHEAD):
+            if t < len(steps):
+                h, unit, pair = steps[t]
+                if pair == 0 and h + 1 < HEADS:
                     dequantise_keys(h + 1, unit)
                     if unit == 0:
                         dequantise_values(h + 1)
-                attend(h, unit)
+                banks.append(score(h, unit, pair))
+            if t >= AHEAD:
+                h, unit, pair = steps[t - AHEAD]
+                if pair == 0:
+                    sums = [sum_banks.tile([P, D + 1], F32, name="sums") for i in range(QUERIES // P)]
+                weigh(h, pair, banks[t - AHEAD], sums)
+                if pair == PAIRS - 1:
+                    finish(h, unit, sums)

@@ -20,10 +20,12 @@ SCALE = 1.0 / math.sqrt(D)
 PIECE = 512
 PIECES = N // PIECE
 BLOCKS = N // P
+PIECE_BLOCKS = PIECE // P
 QUERIES = 256
 UNITS = M // QUERIES
 PAIRS = BLOCKS // 2
-AHEAD = 2
+AHEAD = 3
+LATER = 4
 VD_STEP = D + 16
 
 FLOPS = 2 * 2 * HEADS * D * N * M
@@ -33,10 +35,9 @@ def tile_sfaanetwork_b_kernel(tc, kt, ksc, q, v, vsc, offs, out):
     nc = tc.nc
     with (
         tc.tile_pool(name="held", bufs=1) as held,
-        tc.tile_pool(name="products", bufs=3) as products,
         tc.tile_pool(name="weights", bufs=6) as weights,
         tc.tile_pool(name="results", bufs=4) as results,
-        tc.psum_pool(name="score_banks", bufs=3) as score_banks,
+        tc.psum_pool(name="score_banks", bufs=AHEAD) as score_banks,
         tc.psum_pool(name="sum_banks", bufs=4) as sum_banks,
         tc.psum_pool(name="flip_banks", bufs=1) as flip_banks,
     ):
@@ -44,29 +45,35 @@ def tile_sfaanetwork_b_kernel(tc, kt, ksc, q, v, vsc, offs, out):
         nc.sync.dma_start(offsets[:], offs)
         vsc_sb = held.tile([P, BLOCKS, HEADS], F32, name="vsc_sb")
         v_blocks = v.rearrange("(b p) c -> p b c", p=P)
-        kt_sb, ksc_sb, q_sb, v_sb = [], [], [], []
+        kt_sb = [held.tile([P, S], F32, name=f"kt{h}") for h in range(HEADS)]
+        ksc_sb = [held.tile([P, N], F32, name=f"ksc{h}") for h in range(HEADS)]
+        q_sb = [held.tile([P, M], BF16, name=f"q{h}") for h in range(HEADS)]
+        v_sb = [held.tile([P, BLOCKS, D], F32, name=f"v{h}") for h in range(HEADS)]
         for h in range(HEADS):
             rows = slice(h * D, (h + 1) * D)
-            kt_sb.append(held.tile([P, S], F32, name=f"kt{h}"))
-            ksc_sb.append(held.tile([P, N], F32, name=f"ksc{h}"))
-            q_sb.append(held.tile([P, M], BF16, name=f"q{h}"))
-            v_sb.append(held.tile([P, BLOCKS, D], F32, name=f"v{h}"))
             nc.sync.dma_start(kt_sb[h][:], kt[rows, :])
-            nc.sync.dma_start(ksc_sb[h][:], ksc[rows, :])
-            nc.sync.dma_start(q_sb[h][:], q[rows, :])
-            if h == 0:
-                nc.sync.dma_start(vsc_sb[:], vsc.rearrange("(b p) h -> p b h", p=P))
-            nc.sync.dma_start(v_sb[h][:], v_blocks[:, :, rows])
+            for piece in range(PIECES):
+                cols = slice(piece * PIECE, (piece + 1) * PIECE)
+                blocks = slice(piece * PIECE_BLOCKS, (piece + 1) * PIECE_BLOCKS)
+                nc.sync.dma_start(ksc_sb[h][:, cols], ksc[rows, cols])
+                if piece == 0:
+                    nc.sync.dma_start(q_sb[h][:], q[rows, :])
+                if piece == 0 and h == 0:
+                    nc.sync.dma_start(vsc_sb[:], vsc.rearrange("(b p) h -> p b h", p=P))
+                nc.sync.dma_start(v_sb[h][:, blocks, :], v_blocks[:, blocks, rows])
 
         identity = held.tile([P, P], F32, name="identity")
         make_identity(nc, identity[:])
 
         kd_bf = [held.tile([P, N], BF16, name=f"kd_bf{h}") for h in range(HEADS)]
         vd_one = [held.tile([P, BLOCKS, VD_STEP], BF16, name=f"vd_one{h}") for h in range(HEADS)]
+        for h in range(HEADS):
+            nc.gpsimd.memset(vd_one[h][:, :, D : D + 1], 1.0)
 
-        def dequantise_keys(h, piece):
+        def dequantise(h, piece):
             cols = slice(piece * PIECE, (piece + 1) * PIECE)
-            kd = products.tile([P, PIECE], F32, name="kd")
+            blocks = slice(piece * PIECE_BLOCKS, (piece + 1) * PIECE_BLOCKS)
+            kd = held.tile([P, PIECE], F32, name="kd")
             nc.vector.tensor_tensor(
                 kd[:],
                 kt_sb[h][:].indirect(offsets[:, piece * (PIECE // 16) : (piece + 1) * (PIECE // 16)]),
@@ -74,13 +81,10 @@ def tile_sfaanetwork_b_kernel(tc, kt, ksc, q, v, vsc, offs, out):
                 MULT,
             )
             nc.vector.tensor_copy(kd_bf[h][:, cols], kd[:])
-
-        def dequantise_values(h):
-            nc.gpsimd.memset(vd_one[h][:, :, D : D + 1], 1.0)
             nc.gpsimd.tensor_tensor(
-                vd_one[h][:, :, 0:D],
-                v_sb[h][:],
-                vsc_sb[:, :, h : h + 1].to_broadcast([P, BLOCKS, D]),
+                vd_one[h][:, blocks, 0:D],
+                v_sb[h][:, blocks, :],
+                vsc_sb[:, blocks, h : h + 1].to_broadcast([P, PIECE_BLOCKS, D]),
                 MULT,
             )
 
@@ -98,9 +102,12 @@ def tile_sfaanetwork_b_kernel(tc, kt, ksc, q, v, vsc, offs, out):
                 )
             return scores
 
-        def weigh(h, pair, scores, sums):
+        def exponential(scores):
             e = weights.tile([P, 2, QUERIES], BF16, name="e")
             nc.scalar.activation(out=e[:], in_=scores[:], func=EXP, scale=SCALE)
+            return e
+
+        def accumulate(h, pair, e, sums):
             for k in range(2):
                 block = 2 * pair + k
                 for i in range(QUERIES // P):
@@ -112,38 +119,47 @@ def tile_sfaanetwork_b_kernel(tc, kt, ksc, q, v, vsc, offs, out):
                         stop=(block == BLOCKS - 1),
                     )
 
-        def finish(h, unit, sums):
-            first = unit * QUERIES
-            flipped = flip_banks.tile([P, QUERIES], F32, name="flipped")
+        def divide(sums):
+            quotients = []
             for i in range(QUERIES // P):
                 inverse = results.tile([P, 1], F32, name="inverse")
                 nc.vector.reciprocal(inverse[:], sums[i][:, D : D + 1])
-                normal = results.tile([P, D], F32, name="normal")
-                nc.vector.tensor_scalar_mul(normal[:], sums[i][:, 0:D], inverse[:])
-                nc.tensor.transpose(flipped[:, i * P : (i + 1) * P], normal[:], identity[:])
+                quotient = results.tile([P, D], F32, name="quotient")
+                nc.vector.tensor_scalar_mul(quotient[:], sums[i][:, 0:D], inverse[:])
+                quotients.append(quotient)
+            return quotients
+
+        def flip_and_store(h, unit, quotients):
+            first = unit * QUERIES
+            flipped = flip_banks.tile([P, QUERIES], F32, name="flipped")
+            for i in range(QUERIES // P):
+                nc.tensor.transpose(flipped[:, i * P : (i + 1) * P], quotients[i][:], identity[:])
             answer = results.tile([P, QUERIES], F32, name="answer")
             nc.vector.tensor_copy(answer[:], flipped[:])
             nc.sync.dma_start(out[h * D : (h + 1) * D, first : first + QUERIES], answer[:])
 
         for piece in range(PIECES):
-            dequantise_keys(0, piece)
-        dequantise_values(0)
+            dequantise(0, piece)
 
         steps = [(h, unit, pair) for h in range(HEADS) for unit in range(UNITS) for pair in range(PAIRS)]
-        banks = []
+        banks = {}
         sums = []
-        for t in range(len(steps) + AHEAD):
-            if t < len(steps):
-                h, unit, pair = steps[t]
+        quotients = {}
+        for t in range(-AHEAD, len(steps) + LATER):
+            if 0 <= t < len(steps):
+                e = exponential(banks[t])
+            if t + AHEAD < len(steps):
+                h, unit, pair = steps[t + AHEAD]
                 if pair == 0 and h + 1 < HEADS:
-                    dequantise_keys(h + 1, unit)
-                    if unit == 0:
-                        dequantise_values(h + 1)
-                banks.append(score(h, unit, pair))
-            if t >= AHEAD:
-                h, unit, pair = steps[t - AHEAD]
+                    dequantise(h + 1, unit)
+                banks[t + AHEAD] = score(h, unit, pair)
+            if 0 <= t < len(steps):
+                h, unit, pair = steps[t]
                 if pair == 0:
                     sums = [sum_banks.tile([P, D + 1], F32, name="sums") for i in range(QUERIES // P)]
-                weigh(h, pair, banks[t - AHEAD], sums)
+                accumulate(h, pair, e, sums)
                 if pair == PAIRS - 1:
-                    finish(h, unit, sums)
+                    quotients[t] = divide(sums)
+            if t - LATER in quotients:
+                h, unit, pair = steps[t - LATER]
+                flip_and_store(h, unit, quotients[t - LATER])

@@ -24,7 +24,7 @@ PIECE_BLOCKS = PIECE // P
 QUERIES = 256
 UNITS = M // QUERIES
 PAIRS = BLOCKS // 2
-AHEAD = 3
+AHEAD = 4
 LATER = 4
 VD_STEP = D + 16
 
@@ -39,7 +39,6 @@ def tile_sfaanetwork_b_kernel(tc, kt, ksc, q, v, vsc, offs, out):
         tc.tile_pool(name="results", bufs=4) as results,
         tc.psum_pool(name="score_banks", bufs=AHEAD) as score_banks,
         tc.psum_pool(name="sum_banks", bufs=4) as sum_banks,
-        tc.psum_pool(name="flip_banks", bufs=1) as flip_banks,
     ):
         offsets = held.tile([P, N // 16], U16, name="offsets")
         nc.sync.dma_start(offsets[:], offs)
@@ -131,7 +130,7 @@ def tile_sfaanetwork_b_kernel(tc, kt, ksc, q, v, vsc, offs, out):
 
         def flip_and_store(h, unit, quotients):
             first = unit * QUERIES
-            flipped = flip_banks.tile([P, QUERIES], F32, name="flipped")
+            flipped = sum_banks.tile([P, QUERIES], F32, name="flipped", tag="sums")
             for i in range(QUERIES // P):
                 nc.tensor.transpose(flipped[:, i * P : (i + 1) * P], quotients[i][:], identity[:])
             answer = results.tile([P, QUERIES], F32, name="answer")

@@ -1,7 +1,6 @@
 import math
 
 import concourse.mybir as mybir
-from concourse.masks import make_identity
 
 F32 = mybir.dt.float32
 BF16 = mybir.dt.bfloat16
@@ -25,7 +24,7 @@ QUERIES = 256
 UNITS = M // QUERIES
 PAIRS = BLOCKS // 2
 AHEAD = 4
-LATER = 4
+SQUARE = 32
 VD_STEP = D + 16
 
 FLOPS = 2 * 2 * HEADS * D * N * M
@@ -35,6 +34,7 @@ def tile_sfaanetwork_b_kernel(tc, kt, ksc, q, v, vsc, offs, out):
     nc = tc.nc
     with (
         tc.tile_pool(name="held", bufs=1) as held,
+        tc.tile_pool(name="products", bufs=2) as products,
         tc.tile_pool(name="weights", bufs=6) as weights,
         tc.tile_pool(name="results", bufs=4) as results,
         tc.psum_pool(name="score_banks", bufs=AHEAD) as score_banks,
@@ -61,31 +61,43 @@ def tile_sfaanetwork_b_kernel(tc, kt, ksc, q, v, vsc, offs, out):
                     nc.sync.dma_start(vsc_sb[:], vsc.rearrange("(b p) h -> p b h", p=P))
                 nc.sync.dma_start(v_sb[h][:, blocks, :], v_blocks[:, blocks, rows])
 
-        identity = held.tile([P, P], F32, name="identity")
-        make_identity(nc, identity[:])
+        out_squares = [out[h * D : (h + 1) * D, :].rearrange("(b r) m -> r b m", r=SQUARE) for h in range(HEADS)]
 
         kd_bf = [held.tile([P, N], BF16, name=f"kd_bf{h}") for h in range(HEADS)]
         vd_one = [held.tile([P, BLOCKS, VD_STEP], BF16, name=f"vd_one{h}") for h in range(HEADS)]
         for h in range(HEADS):
             nc.gpsimd.memset(vd_one[h][:, :, D : D + 1], 1.0)
 
-        def dequantise(h, piece):
-            cols = slice(piece * PIECE, (piece + 1) * PIECE)
-            blocks = slice(piece * PIECE_BLOCKS, (piece + 1) * PIECE_BLOCKS)
-            kd = held.tile([P, PIECE], F32, name="kd")
+        def look_up(h, piece):
+            kd = products.tile([P, PIECE], F32, name="kd")
             nc.vector.tensor_tensor(
                 kd[:],
                 kt_sb[h][:].indirect(offsets[:, piece * (PIECE // 16) : (piece + 1) * (PIECE // 16)]),
-                ksc_sb[h][:, cols],
+                ksc_sb[h][:, piece * PIECE : (piece + 1) * PIECE],
                 MULT,
             )
-            nc.vector.tensor_copy(kd_bf[h][:, cols], kd[:])
+            return kd
+
+        def round_keys(h, piece, kd):
+            nc.vector.tensor_copy(kd_bf[h][:, piece * PIECE : (piece + 1) * PIECE], kd[:])
+
+        def scale_values(h, piece):
+            blocks = slice(piece * PIECE_BLOCKS, (piece + 1) * PIECE_BLOCKS)
             nc.gpsimd.tensor_tensor(
                 vd_one[h][:, blocks, 0:D],
                 v_sb[h][:, blocks, :],
                 vsc_sb[:, blocks, h : h + 1].to_broadcast([P, PIECE_BLOCKS, D]),
                 MULT,
             )
+
+        pieces = [(h, piece) for h in range(HEADS) for piece in range(PIECES)]
+        looked_up = {0: look_up(0, 0)}
+
+        def prepare(n):
+            if n + 1 < len(pieces):
+                looked_up[n + 1] = look_up(pieces[n + 1][0], pieces[n + 1][1])
+            round_keys(pieces[n][0], pieces[n][1], looked_up[n])
+            scale_values(pieces[n][0], pieces[n][1])
 
         def score(h, unit, pair):
             first = unit * QUERIES
@@ -118,39 +130,38 @@ def tile_sfaanetwork_b_kernel(tc, kt, ksc, q, v, vsc, offs, out):
                         stop=(block == BLOCKS - 1),
                     )
 
-        def divide(sums):
-            quotients = []
+        def finish(h, unit, sums):
+            first = unit * QUERIES
+            quotient = results.tile([P, QUERIES], F32, name="quotient", align_bytes=64)
             for i in range(QUERIES // P):
                 inverse = results.tile([P, 1], F32, name="inverse")
                 nc.vector.reciprocal(inverse[:], sums[i][:, D : D + 1])
-                quotient = results.tile([P, D], F32, name="quotient")
-                nc.vector.tensor_scalar_mul(quotient[:], sums[i][:, 0:D], inverse[:])
-                quotients.append(quotient)
-            return quotients
+                nc.vector.tensor_scalar_mul(quotient[:, i * D : (i + 1) * D], sums[i][:, 0:D], inverse[:])
+            flipped = results.tile([P, QUERIES], F32, name="flipped", align_bytes=64)
+            nc.vector.transpose(flipped[:], quotient[:])
+            for a in range(P // SQUARE):
+                for i in range(QUERIES // P):
+                    column = first + i * P + a * SQUARE
+                    nc.sync.dma_start(
+                        out_squares[h][:, :, column : column + SQUARE],
+                        flipped[a * SQUARE : (a + 1) * SQUARE, i * D : (i + 1) * D].rearrange(
+                            "r (b c) -> r b c", c=SQUARE
+                        ),
+                    )
 
-        def flip_and_store(h, unit, quotients):
-            first = unit * QUERIES
-            flipped = sum_banks.tile([P, QUERIES], F32, name="flipped", tag="sums")
-            for i in range(QUERIES // P):
-                nc.tensor.transpose(flipped[:, i * P : (i + 1) * P], quotients[i][:], identity[:])
-            answer = results.tile([P, QUERIES], F32, name="answer")
-            nc.vector.tensor_copy(answer[:], flipped[:])
-            nc.sync.dma_start(out[h * D : (h + 1) * D, first : first + QUERIES], answer[:])
-
-        for piece in range(PIECES):
-            dequantise(0, piece)
+        for n in range(PIECES):
+            prepare(n)
 
         steps = [(h, unit, pair) for h in range(HEADS) for unit in range(UNITS) for pair in range(PAIRS)]
         banks = {}
         sums = []
-        quotients = {}
-        for t in range(-AHEAD, len(steps) + LATER):
+        for t in range(-AHEAD, len(steps)):
             if 0 <= t < len(steps):
                 e = exponential(banks[t])
             if t + AHEAD < len(steps):
                 h, unit, pair = steps[t + AHEAD]
                 if pair == 0 and h + 1 < HEADS:
-                    dequantise(h + 1, unit)
+                    prepare((h + 1) * PIECES + unit)
                 banks[t + AHEAD] = score(h, unit, pair)
             if 0 <= t < len(steps):
                 h, unit, pair = steps[t]
@@ -158,7 +169,4 @@ def tile_sfaanetwork_b_kernel(tc, kt, ksc, q, v, vsc, offs, out):
                     sums = [sum_banks.tile([P, D + 1], F32, name="sums") for i in range(QUERIES // P)]
                 accumulate(h, pair, e, sums)
                 if pair == PAIRS - 1:
-                    quotients[t] = divide(sums)
-            if t - LATER in quotients:
-                h, unit, pair = steps[t - LATER]
-                flip_and_store(h, unit, quotients[t - LATER])
+                    finish(h, unit, sums)

@@ -105,7 +105,7 @@ def tile_sfaanetwork_b_kernel(tc, kt, ksc, q, v, vsc, offs, out):
             for k in range(2):
                 block = 2 * pair + k
                 nc.tensor.matmul(
-                    scores[:, k, :],
+                    scores[:, k, :].rearrange("p (i a c) -> p a i c", i=QUERIES // P, c=SQUARE),
                     lhsT=kd_bf[h][:, block * P : (block + 1) * P],
                     rhs=q_sb[h][:, first : first + QUERIES],
                     start=True,
@@ -132,22 +132,24 @@ def tile_sfaanetwork_b_kernel(tc, kt, ksc, q, v, vsc, offs, out):
 
         def finish(h, unit, sums):
             first = unit * QUERIES
+            blocks = QUERIES // P
             quotient = results.tile([P, QUERIES], F32, name="quotient", align_bytes=64)
-            for i in range(QUERIES // P):
+            for i in range(blocks):
                 inverse = results.tile([P, 1], F32, name="inverse")
                 nc.vector.reciprocal(inverse[:], sums[i][:, D : D + 1])
-                nc.vector.tensor_scalar_mul(quotient[:, i * D : (i + 1) * D], sums[i][:, 0:D], inverse[:])
+                nc.vector.tensor_scalar_mul(
+                    quotient[:].rearrange("p (b i r) -> p i b r", i=blocks, r=SQUARE)[:, i],
+                    sums[i][:, 0:D].rearrange("p (b r) -> p b r", r=SQUARE),
+                    inverse[:],
+                )
             flipped = results.tile([P, QUERIES], F32, name="flipped", align_bytes=64)
             nc.vector.transpose(flipped[:], quotient[:])
             for a in range(P // SQUARE):
-                for i in range(QUERIES // P):
-                    column = first + i * P + a * SQUARE
-                    nc.sync.dma_start(
-                        out_squares[h][:, :, column : column + SQUARE],
-                        flipped[a * SQUARE : (a + 1) * SQUARE, i * D : (i + 1) * D].rearrange(
-                            "r (b c) -> r b c", c=SQUARE
-                        ),
-                    )
+                column = first + a * blocks * SQUARE
+                nc.sync.dma_start(
+                    out_squares[h][:, :, column : column + blocks * SQUARE],
+                    flipped[a * SQUARE : (a + 1) * SQUARE, :].rearrange("r (b n) -> r b n", n=blocks * SQUARE),
+                )
 
         for n in range(PIECES):
             prepare(n)

@@ -43,6 +43,7 @@ def tile_sfaanetwork_b_kernel(tc, kt, ksc, q, v, vsc, offs, out):
         offsets = held.tile([P, N // 16], U16, name="offsets")
         nc.sync.dma_start(offsets[:], offs)
         vsc_sb = held.tile([P, BLOCKS, HEADS], F32, name="vsc_sb")
+        nc.gpsimd.dma_start(vsc_sb[:], vsc.rearrange("(b p) h -> p b h", p=P))
         v_blocks = v.rearrange("(b p) c -> p b c", p=P)
         kt_sb = [held.tile([P, S], F32, name=f"kt{h}") for h in range(HEADS)]
         ksc_sb = [held.tile([P, N], F32, name=f"ksc{h}") for h in range(HEADS)]
@@ -57,8 +58,6 @@ def tile_sfaanetwork_b_kernel(tc, kt, ksc, q, v, vsc, offs, out):
                 nc.sync.dma_start(ksc_sb[h][:, cols], ksc[rows, cols])
                 if piece == 0:
                     nc.sync.dma_start(q_sb[h][:], q[rows, :])
-                if piece == 0 and h == 0:
-                    nc.sync.dma_start(vsc_sb[:], vsc.rearrange("(b p) h -> p b h", p=P))
                 nc.sync.dma_start(v_sb[h][:, blocks, :], v_blocks[:, blocks, rows])
 
         out_squares = [out[h * D : (h + 1) * D, :].rearrange("(b r) m -> r b m", r=SQUARE) for h in range(HEADS)]

@@ -82,7 +82,7 @@ def tile_sfaanetwork_b_kernel(tc, kt, ksc, q, v, vsc, offs, out):
 
         def scale_values(h, piece):
             blocks = slice(piece * PIECE_BLOCKS, (piece + 1) * PIECE_BLOCKS)
-            nc.gpsimd.tensor_tensor(
+            nc.vector.tensor_tensor(
                 vd_one[h][:, blocks, 0:D],
                 v_sb[h][:, blocks, :],
                 vsc_sb[:, blocks, h : h + 1].to_broadcast([P, PIECE_BLOCKS, D]),

@@ -43,8 +43,8 @@ def tile_sfaanetwork_b_kernel(tc, kt, ksc, q, v, vsc, offs, out):
         offsets = held.tile([P, N // 16], U16, name="offsets")
         nc.sync.dma_start(offsets[:], offs)
         vsc_sb = held.tile([P, BLOCKS, HEADS], F32, name="vsc_sb")
-        nc.gpsimd.dma_start(vsc_sb[:], vsc.rearrange("(b p) h -> p b h", p=P))
         v_blocks = v.rearrange("(b p) c -> p b c", p=P)
+        vsc_blocks = vsc.rearrange("(b p) h -> p b h", p=P)
         kt_sb = [held.tile([P, S], F32, name=f"kt{h}") for h in range(HEADS)]
         ksc_sb = [held.tile([P, N], F32, name=f"ksc{h}") for h in range(HEADS)]
         q_sb = [held.tile([P, M], BF16, name=f"q{h}") for h in range(HEADS)]
@@ -58,6 +58,8 @@ def tile_sfaanetwork_b_kernel(tc, kt, ksc, q, v, vsc, offs, out):
                 nc.sync.dma_start(ksc_sb[h][:, cols], ksc[rows, cols])
                 if piece == 0:
                     nc.sync.dma_start(q_sb[h][:], q[rows, :])
+                if h == 0:
+                    nc.sync.dma_start(vsc_sb[:, blocks, :], vsc_blocks[:, blocks, :])
                 nc.sync.dma_start(v_sb[h][:, blocks, :], v_blocks[:, blocks, rows])
 
         out_squares = [out[h * D : (h + 1) * D, :].rearrange("(b r) m -> r b m", r=SQUARE) for h in range(HEADS)]
@@ -90,13 +92,12 @@ def tile_sfaanetwork_b_kernel(tc, kt, ksc, q, v, vsc, offs, out):
             )
 
         pieces = [(h, piece) for h in range(HEADS) for piece in range(PIECES)]
-        looked_up = {0: look_up(0, 0)}
 
         def prepare(n):
-            if n + 1 < len(pieces):
-                looked_up[n + 1] = look_up(pieces[n + 1][0], pieces[n + 1][1])
-            round_keys(pieces[n][0], pieces[n][1], looked_up[n])
-            scale_values(pieces[n][0], pieces[n][1])
+            h, piece = pieces[n]
+            kd = look_up(h, piece)
+            scale_values(h, piece)
+            round_keys(h, piece, kd)
 
         def score(h, unit, pair):
             first = unit * QUERIES
@@ -150,24 +151,31 @@ def tile_sfaanetwork_b_kernel(tc, kt, ksc, q, v, vsc, offs, out):
                     flipped[a * SQUARE : (a + 1) * SQUARE, :].rearrange("r (b n) -> r b n", n=blocks * SQUARE),
                 )
 
-        for n in range(PIECES):
+        for n in range(PIECES + 1):
             prepare(n)
 
-        steps = [(h, unit, pair) for h in range(HEADS) for unit in range(UNITS) for pair in range(PAIRS)]
+        piece_pairs = PAIRS // PIECES
+        steps = [
+            (0, unit, piece * piece_pairs + k) for piece in range(PIECES) for unit in range(2) for k in range(piece_pairs)
+        ]
+        steps += [(0, unit, pair) for unit in range(2, UNITS) for pair in range(PAIRS)]
+        steps += [(h, unit, pair) for h in range(1, HEADS) for unit in range(UNITS) for pair in range(PAIRS)]
+
         banks = {}
-        sums = []
+        sums = {}
         for t in range(-AHEAD, len(steps)):
             if 0 <= t < len(steps):
                 e = exponential(banks[t])
             if t + AHEAD < len(steps):
                 h, unit, pair = steps[t + AHEAD]
-                if pair == 0 and h + 1 < HEADS:
-                    prepare((h + 1) * PIECES + unit)
                 banks[t + AHEAD] = score(h, unit, pair)
             if 0 <= t < len(steps):
                 h, unit, pair = steps[t]
                 if pair == 0:
-                    sums = [sum_banks.tile([P, D + 1], F32, name="sums") for i in range(QUERIES // P)]
-                accumulate(h, pair, e, sums)
+                    sums[unit] = [sum_banks.tile([P, D + 1], F32, name="sums") for i in range(QUERIES // P)]
+                accumulate(h, pair, e, sums[unit])
                 if pair == PAIRS - 1:
-                    finish(h, unit, sums)
+                    finish(h, unit, sums[unit])
+                    n = PIECES + 1 + h * UNITS + unit
+                    if n < len(pieces):
+                        prepare(n)

@@ -20,9 +20,9 @@ PIECE = 512
 PIECES = N // PIECE
 BLOCKS = N // P
 PIECE_BLOCKS = PIECE // P
-QUERIES = 256
+QUERIES = 512
+QUERY_BLOCKS = QUERIES // P
 UNITS = M // QUERIES
-PAIRS = BLOCKS // 2
 AHEAD = 4
 SQUARE = 32
 VD_STEP = D + 16
@@ -36,7 +36,7 @@ def tile_sfaanetwork_b_kernel(tc, kt, ksc, q, v, vsc, offs, out):
         tc.tile_pool(name="held", bufs=1) as held,
         tc.tile_pool(name="products", bufs=2) as products,
         tc.tile_pool(name="weights", bufs=6) as weights,
-        tc.tile_pool(name="results", bufs=4) as results,
+        tc.tile_pool(name="results", bufs=2) as results,
         tc.psum_pool(name="score_banks", bufs=AHEAD) as score_banks,
         tc.psum_pool(name="sum_banks", bufs=4) as sum_banks,
     ):
@@ -99,83 +99,74 @@ def tile_sfaanetwork_b_kernel(tc, kt, ksc, q, v, vsc, offs, out):
             scale_values(h, piece)
             round_keys(h, piece, kd)
 
-        def score(h, unit, pair):
+        def score(h, unit, block):
             first = unit * QUERIES
-            scores = score_banks.tile([P, 2, QUERIES], F32, name="scores")
-            for k in range(2):
-                block = 2 * pair + k
-                nc.tensor.matmul(
-                    scores[:, k, :].rearrange("p (i a c) -> p a i c", i=QUERIES // P, c=SQUARE),
-                    lhsT=kd_bf[h][:, block * P : (block + 1) * P],
-                    rhs=q_sb[h][:, first : first + QUERIES],
-                    start=True,
-                    stop=True,
-                )
+            scores = score_banks.tile([P, QUERIES], F32, name="scores")
+            nc.tensor.matmul(
+                scores[:].rearrange("p (i a c) -> p a i c", i=QUERY_BLOCKS, c=SQUARE),
+                lhsT=kd_bf[h][:, block * P : (block + 1) * P],
+                rhs=q_sb[h][:, first : first + QUERIES],
+                start=True,
+                stop=True,
+            )
             return scores
 
         def exponential(scores):
-            e = weights.tile([P, 2, QUERIES], BF16, name="e")
+            e = weights.tile([P, QUERIES], BF16, name="e")
             nc.scalar.activation(out=e[:], in_=scores[:], func=EXP, scale=SCALE)
             return e
 
-        def accumulate(h, pair, e, sums):
-            for k in range(2):
-                block = 2 * pair + k
-                for i in range(QUERIES // P):
-                    nc.tensor.matmul(
-                        sums[i][:],
-                        lhsT=e[:, k, i * P : (i + 1) * P],
-                        rhs=vd_one[h][:, block, 0 : D + 1],
-                        start=(block == 0),
-                        stop=(block == BLOCKS - 1),
-                    )
+        def accumulate(h, block, e, sums):
+            for i in range(QUERY_BLOCKS):
+                nc.tensor.matmul(
+                    sums[i // 2][:, i % 2, 0 : D + 1],
+                    lhsT=e[:, i * P : (i + 1) * P],
+                    rhs=vd_one[h][:, block, 0 : D + 1],
+                    start=(block == 0 and i % 2 == 0),
+                    stop=(block == BLOCKS - 1 and i % 2 == 1),
+                )
 
         def finish(h, unit, sums):
             first = unit * QUERIES
-            blocks = QUERIES // P
             quotient = results.tile([P, QUERIES], F32, name="quotient", align_bytes=64)
-            for i in range(blocks):
-                inverse = results.tile([P, 1], F32, name="inverse")
-                nc.vector.reciprocal(inverse[:], sums[i][:, D : D + 1])
-                nc.vector.tensor_scalar_mul(
-                    quotient[:].rearrange("p (b i r) -> p i b r", i=blocks, r=SQUARE)[:, i],
-                    sums[i][:, 0:D].rearrange("p (b r) -> p b r", r=SQUARE),
-                    inverse[:],
+            by_query_block = quotient[:].rearrange("p (b i r) -> p i b r", i=QUERY_BLOCKS, r=SQUARE)
+            for w in range(QUERY_BLOCKS // 2):
+                inverse = results.tile([P, 2, 1, 1], F32, name="inverse")
+                nc.vector.reciprocal(inverse[:, :, :, 0], sums[w][:, :, D : D + 1])
+                nc.vector.tensor_tensor(
+                    by_query_block[:, 2 * w : 2 * w + 2],
+                    sums[w][:, :, 0:D].rearrange("p k (b r) -> p k b r", r=SQUARE),
+                    inverse[:].to_broadcast([P, 2, D // SQUARE, SQUARE]),
+                    MULT,
                 )
             flipped = results.tile([P, QUERIES], F32, name="flipped", align_bytes=64)
             nc.vector.transpose(flipped[:], quotient[:])
             for a in range(P // SQUARE):
-                column = first + a * blocks * SQUARE
+                column = first + a * P
                 nc.sync.dma_start(
-                    out_squares[h][:, :, column : column + blocks * SQUARE],
-                    flipped[a * SQUARE : (a + 1) * SQUARE, :].rearrange("r (b n) -> r b n", n=blocks * SQUARE),
+                    out_squares[h][:, :, column : column + P],
+                    flipped[a * SQUARE : (a + 1) * SQUARE, :].rearrange("r (b n) -> r b n", n=P),
                 )
 
-        for n in range(PIECES + 1):
+        for n in range(PIECES):
             prepare(n)
 
-        piece_pairs = PAIRS // PIECES
-        steps = [
-            (0, unit, piece * piece_pairs + k) for piece in range(PIECES) for unit in range(2) for k in range(piece_pairs)
-        ]
-        steps += [(0, unit, pair) for unit in range(2, UNITS) for pair in range(PAIRS)]
-        steps += [(h, unit, pair) for h in range(1, HEADS) for unit in range(UNITS) for pair in range(PAIRS)]
-
+        steps = [(h, unit, block) for h in range(HEADS) for unit in range(UNITS) for block in range(BLOCKS)]
+        steps_to_a_piece = UNITS * BLOCKS // PIECES
         banks = {}
-        sums = {}
+        sums = []
         for t in range(-AHEAD, len(steps)):
             if 0 <= t < len(steps):
                 e = exponential(banks[t])
             if t + AHEAD < len(steps):
-                h, unit, pair = steps[t + AHEAD]
-                banks[t + AHEAD] = score(h, unit, pair)
+                h, unit, block = steps[t + AHEAD]
+                banks[t + AHEAD] = score(h, unit, block)
             if 0 <= t < len(steps):
-                h, unit, pair = steps[t]
-                if pair == 0:
-                    sums[unit] = [sum_banks.tile([P, D + 1], F32, name="sums") for i in range(QUERIES // P)]
-                accumulate(h, pair, e, sums[unit])
-                if pair == PAIRS - 1:
-                    finish(h, unit, sums[unit])
-                    n = PIECES + 1 + h * UNITS + unit
-                    if n < len(pieces):
-                        prepare(n)
+                h, unit, block = steps[t]
+                if block == 0:
+                    sums = [sum_banks.tile([P, 2, 2 * D], F32, name="sums") for w in range(QUERY_BLOCKS // 2)]
+                accumulate(h, block, e, sums)
+                if block == BLOCKS - 1:
+                    finish(h, unit, sums)
+                if t % steps_to_a_piece == 0 and PIECES + t // steps_to_a_piece < len(pieces):
+                    prepare(PIECES + t // steps_to_a_piece)

@@ -7,6 +7,7 @@ BF16 = mybir.dt.bfloat16
 U16 = mybir.dt.uint16
 MULT = mybir.AluOpType.mult
 EXP = mybir.ActivationFunctionType.Exp
+COPY = mybir.ActivationFunctionType.Copy
 
 P = 128
 HEADS = 4
@@ -17,9 +18,7 @@ M = 1024
 SCALE = 1.0 / math.sqrt(D)
 
 PIECE = 512
-PIECES = N // PIECE
 BLOCKS = N // P
-PIECE_BLOCKS = PIECE // P
 QUERIES = 512
 QUERY_BLOCKS = QUERIES // P
 UNITS = M // QUERIES
@@ -52,11 +51,11 @@ def tile_sfaanetwork_b_kernel(tc, kt, ksc, q, v, vsc, offs, out):
         for h in range(HEADS):
             rows = slice(h * D, (h + 1) * D)
             nc.sync.dma_start(kt_sb[h][:], kt[rows, :])
-            for piece in range(PIECES):
-                cols = slice(piece * PIECE, (piece + 1) * PIECE)
-                blocks = slice(piece * PIECE_BLOCKS, (piece + 1) * PIECE_BLOCKS)
+            for first in range(0, N, PIECE):
+                cols = slice(first, first + PIECE)
+                blocks = slice(first // P, (first + PIECE) // P)
                 nc.sync.dma_start(ksc_sb[h][:, cols], ksc[rows, cols])
-                if piece == 0:
+                if first == 0:
                     nc.sync.dma_start(q_sb[h][:], q[rows, :])
                 if h == 0:
                     nc.sync.dma_start(vsc_sb[:, blocks, :], vsc_blocks[:, blocks, :])
@@ -69,35 +68,45 @@ def tile_sfaanetwork_b_kernel(tc, kt, ksc, q, v, vsc, offs, out):
         for h in range(HEADS):
             nc.gpsimd.memset(vd_one[h][:, :, D : D + 1], 1.0)
 
-        def look_up(h, piece):
-            kd = products.tile([P, PIECE], F32, name="kd")
+        def look_up(h, first, count):
+            kd = products.tile([P, count], F32, name="kd")
             nc.vector.tensor_tensor(
                 kd[:],
-                kt_sb[h][:].indirect(offsets[:, piece * (PIECE // 16) : (piece + 1) * (PIECE // 16)]),
-                ksc_sb[h][:, piece * PIECE : (piece + 1) * PIECE],
+                kt_sb[h][:].indirect(offsets[:, first // 16 : (first + count) // 16]),
+                ksc_sb[h][:, first : first + count],
                 MULT,
             )
             return kd
 
-        def round_keys(h, piece, kd):
-            nc.vector.tensor_copy(kd_bf[h][:, piece * PIECE : (piece + 1) * PIECE], kd[:])
+        def round_keys(h, first, count, kd):
+            nc.vector.tensor_copy(kd_bf[h][:, first : first + count], kd[:])
 
-        def scale_values(h, piece):
-            blocks = slice(piece * PIECE_BLOCKS, (piece + 1) * PIECE_BLOCKS)
+        def scale_values(h, first, count):
+            blocks = slice(first // P, (first + count) // P)
             nc.vector.tensor_tensor(
                 vd_one[h][:, blocks, 0:D],
                 v_sb[h][:, blocks, :],
-                vsc_sb[:, blocks, h : h + 1].to_broadcast([P, PIECE_BLOCKS, D]),
+                vsc_sb[:, blocks, h : h + 1].to_broadcast([P, count // P, D]),
                 MULT,
             )
 
-        pieces = [(h, piece) for h in range(HEADS) for piece in range(PIECES)]
+        def scale_values_early(h, first, count):
+            for block in range(first // P, (first + count) // P):
+                nc.scalar.activation(
+                    out=vd_one[h][:, block, 0:D], in_=v_sb[h][:, block, :], func=COPY, scale=vsc_sb[:, block, h : h + 1]
+                )
+
+        halves = [(0, 0, PIECE // 2), (0, PIECE // 2, PIECE // 2)]
+        pieces = halves + [(h, first, PIECE) for h in range(HEADS) for first in range(0, N, PIECE)][1:]
 
         def prepare(n):
-            h, piece = pieces[n]
-            kd = look_up(h, piece)
-            scale_values(h, piece)
-            round_keys(h, piece, kd)
+            h, first, count = pieces[n]
+            kd = look_up(h, first, count)
+            if n < len(halves):
+                scale_values_early(h, first, count)
+            else:
+                scale_values(h, first, count)
+            round_keys(h, first, count, kd)
 
         def score(h, unit, block):
             first = unit * QUERIES
@@ -148,11 +157,12 @@ def tile_sfaanetwork_b_kernel(tc, kt, ksc, q, v, vsc, offs, out):
                     flipped[a * SQUARE : (a + 1) * SQUARE, :].rearrange("r (b n) -> r b n", n=P),
                 )
 
-        for n in range(PIECES):
+        first_pieces = N // PIECE + 1
+        for n in range(first_pieces):
             prepare(n)
 
         steps = [(h, unit, block) for h in range(HEADS) for unit in range(UNITS) for block in range(BLOCKS)]
-        steps_to_a_piece = UNITS * BLOCKS // PIECES
+        steps_to_a_piece = UNITS * BLOCKS // (N // PIECE)
         banks = {}
         sums = []
         for t in range(-AHEAD, len(steps)):
@@ -168,5 +178,5 @@ def tile_sfaanetwork_b_kernel(tc, kt, ksc, q, v, vsc, offs, out):
                 accumulate(h, block, e, sums)
                 if block == BLOCKS - 1:
                     finish(h, unit, sums)
-                if t % steps_to_a_piece == 0 and PIECES + t // steps_to_a_piece < len(pieces):
-                    prepare(PIECES + t // steps_to_a_piece)
+                if t % steps_to_a_piece == 0 and first_pieces + t // steps_to_a_piece < len(pieces):
+                    prepare(first_pieces + t // steps_to_a_piece)

@@ -51,12 +51,19 @@ def tile_sfaanetwork_b_kernel(tc, kt, ksc, q, v, vsc, offs, out):
         for h in range(HEADS):
             rows = slice(h * D, (h + 1) * D)
             nc.sync.dma_start(kt_sb[h][:], kt[rows, :])
+            if h == 0:
+                nc.sync.dma_start(ksc_sb[h][:, 0 : PIECE // 2], ksc[rows, 0 : PIECE // 2])
+                nc.sync.dma_start(q_sb[h][:, 0:QUERIES], q[rows, 0:QUERIES])
+                nc.sync.dma_start(ksc_sb[h][:, PIECE // 2 : PIECE], ksc[rows, PIECE // 2 : PIECE])
             for first in range(0, N, PIECE):
                 cols = slice(first, first + PIECE)
                 blocks = slice(first // P, (first + PIECE) // P)
-                nc.sync.dma_start(ksc_sb[h][:, cols], ksc[rows, cols])
-                if first == 0:
+                if h > 0 or first > 0:
+                    nc.sync.dma_start(ksc_sb[h][:, cols], ksc[rows, cols])
+                if h > 0 and first == 0:
                     nc.sync.dma_start(q_sb[h][:], q[rows, :])
+                if h == 0 and first == 0:
+                    nc.sync.dma_start(q_sb[h][:, QUERIES:M], q[rows, QUERIES:M])
                 if h == 0:
                     nc.sync.dma_start(vsc_sb[:, blocks, :], vsc_blocks[:, blocks, :])
                 nc.sync.dma_start(v_sb[h][:, blocks, :], v_blocks[:, blocks, rows])
@@ -161,10 +168,16 @@ def tile_sfaanetwork_b_kernel(tc, kt, ksc, q, v, vsc, offs, out):
         for n in range(first_pieces):
             prepare(n)
 
-        steps = [(h, unit, block) for h in range(HEADS) for unit in range(UNITS) for block in range(BLOCKS)]
+        steps = [
+            (0, unit, block)
+            for first in range(0, BLOCKS, PIECE // P)
+            for unit in range(UNITS)
+            for block in range(first, first + PIECE // P)
+        ]
+        steps += [(h, unit, block) for h in range(1, HEADS) for unit in range(UNITS) for block in range(BLOCKS)]
         steps_to_a_piece = UNITS * BLOCKS // (N // PIECE)
         banks = {}
-        sums = []
+        sums = {}
         for t in range(-AHEAD, len(steps)):
             if 0 <= t < len(steps):
                 e = exponential(banks[t])
@@ -174,9 +187,9 @@ def tile_sfaanetwork_b_kernel(tc, kt, ksc, q, v, vsc, offs, out):
             if 0 <= t < len(steps):
                 h, unit, block = steps[t]
                 if block == 0:
-                    sums = [sum_banks.tile([P, 2, 2 * D], F32, name="sums") for w in range(QUERY_BLOCKS // 2)]
-                accumulate(h, block, e, sums)
+                    sums[unit] = [sum_banks.tile([P, 2, 2 * D], F32, name="sums") for w in range(QUERY_BLOCKS // 2)]
+                accumulate(h, block, e, sums[unit])
                 if block == BLOCKS - 1:
-                    finish(h, unit, sums)
+                    finish(h, unit, sums[unit])
                 if t % steps_to_a_piece == 0 and first_pieces + t // steps_to_a_piece < len(pieces):
                     prepare(first_pieces + t // steps_to_a_piece)

@@ -41,7 +41,7 @@ def tile_sfaanetwork_b_kernel(tc, kt, ksc, q, v, vsc, offs, out):
     ):
         offsets = held.tile([P, N // 16], U16, name="offsets")
         nc.sync.dma_start(offsets[:], offs)
-        vsc_sb = held.tile([P, BLOCKS, HEADS], F32, name="vsc_sb")
+        vsc_sb = held.tile([P, BLOCKS, 2 * HEADS], F32, name="vsc_sb")
         v_blocks = v.rearrange("(b p) c -> p b c", p=P)
         vsc_blocks = vsc.rearrange("(b p) h -> p b h", p=P)
         kt_sb = [held.tile([P, S], F32, name=f"kt{h}") for h in range(HEADS)]
@@ -60,13 +60,13 @@ def tile_sfaanetwork_b_kernel(tc, kt, ksc, q, v, vsc, offs, out):
                 blocks = slice(first // P, (first + PIECE) // P)
                 if h > 0 or first > 0:
                     nc.sync.dma_start(ksc_sb[h][:, cols], ksc[rows, cols])
-                if h > 0 and first == 0:
-                    nc.sync.dma_start(q_sb[h][:], q[rows, :])
                 if h == 0 and first == 0:
                     nc.sync.dma_start(q_sb[h][:, QUERIES:M], q[rows, QUERIES:M])
                 if h == 0:
-                    nc.sync.dma_start(vsc_sb[:, blocks, :], vsc_blocks[:, blocks, :])
+                    nc.sync.dma_start(vsc_sb[:, blocks, 0:HEADS], vsc_blocks[:, blocks, :])
                 nc.sync.dma_start(v_sb[h][:, blocks, :], v_blocks[:, blocks, rows])
+                if h > 0 and first == 0:
+                    nc.sync.dma_start(q_sb[h][:], q[rows, :])
 
         out_squares = [out[h * D : (h + 1) * D, :].rearrange("(b r) m -> r b m", r=SQUARE) for h in range(HEADS)]
 

@@ -19,9 +19,8 @@ SCALE = 1.0 / math.sqrt(D)
 
 PIECE = 512
 BLOCKS = N // P
+BANK = 512
 QUERIES = 512
-QUERY_BLOCKS = QUERIES // P
-UNITS = M // QUERIES
 AHEAD = 4
 SQUARE = 32
 VD_STEP = D + 16
@@ -115,38 +114,40 @@ def tile_sfaanetwork_b_kernel(tc, kt, ksc, q, v, vsc, offs, out):
                 scale_values(h, first, count)
             round_keys(h, first, count, kd)
 
-        def score(h, unit, block):
-            first = unit * QUERIES
-            scores = score_banks.tile([P, QUERIES], F32, name="scores")
-            nc.tensor.matmul(
-                scores[:].rearrange("p (i a c) -> p a i c", i=QUERY_BLOCKS, c=SQUARE),
-                lhsT=kd_bf[h][:, block * P : (block + 1) * P],
-                rhs=q_sb[h][:, first : first + QUERIES],
-                start=True,
-                stop=True,
-            )
+        def score(h, first, queries, block):
+            scores = score_banks.tile([P, BANK // queries, queries], F32, name="scores")
+            for k in range(BANK // queries):
+                nc.tensor.matmul(
+                    scores[:, k, :].rearrange("p (i a c) -> p a i c", i=queries // P, c=SQUARE),
+                    lhsT=kd_bf[h][:, (block + k) * P : (block + k + 1) * P],
+                    rhs=q_sb[h][:, first : first + queries],
+                    start=True,
+                    stop=True,
+                )
             return scores
 
-        def exponential(scores):
-            e = weights.tile([P, QUERIES], BF16, name="e")
+        def exponential(scores, queries):
+            e = weights.tile([P, BANK // queries, queries], BF16, name="e")
             nc.scalar.activation(out=e[:], in_=scores[:], func=EXP, scale=SCALE)
             return e
 
-        def accumulate(h, block, e, sums):
-            for i in range(QUERY_BLOCKS):
-                nc.tensor.matmul(
-                    sums[i // 2][:, i % 2, 0 : D + 1],
-                    lhsT=e[:, i * P : (i + 1) * P],
-                    rhs=vd_one[h][:, block, 0 : D + 1],
-                    start=(block == 0 and i % 2 == 0),
-                    stop=(block == BLOCKS - 1 and i % 2 == 1),
-                )
+        def accumulate(h, queries, block, e, sums):
+            for k in range(BANK // queries):
+                for i in range(queries // P):
+                    nc.tensor.matmul(
+                        sums[i // 2][:, i % 2, 0 : D + 1],
+                        lhsT=e[:, k, i * P : (i + 1) * P],
+                        rhs=vd_one[h][:, block + k, 0 : D + 1],
+                        start=(block + k == 0 and i % 2 == 0),
+                        stop=(block + k == BLOCKS - 1 and i % 2 == 1),
+                    )
 
-        def finish(h, unit, sums):
-            first = unit * QUERIES
-            quotient = results.tile([P, QUERIES], F32, name="quotient", align_bytes=64)
-            by_query_block = quotient[:].rearrange("p (b i r) -> p i b r", i=QUERY_BLOCKS, r=SQUARE)
-            for w in range(QUERY_BLOCKS // 2):
+        def finish(h, first, queries, sums):
+            query_blocks = queries // P
+            run = query_blocks * SQUARE
+            quotient = results.tile([P, queries], F32, name="quotient", align_bytes=64)
+            by_query_block = quotient[:].rearrange("p (b i r) -> p i b r", i=query_blocks, r=SQUARE)
+            for w in range(query_blocks // 2):
                 inverse = results.tile([P, 2, 1, 1], F32, name="inverse")
                 nc.vector.reciprocal(inverse[:, :, :, 0], sums[w][:, :, D : D + 1])
                 nc.vector.tensor_tensor(
@@ -155,41 +156,42 @@ def tile_sfaanetwork_b_kernel(tc, kt, ksc, q, v, vsc, offs, out):
                     inverse[:].to_broadcast([P, 2, D // SQUARE, SQUARE]),
                     MULT,
                 )
-            flipped = results.tile([P, QUERIES], F32, name="flipped", align_bytes=64)
+            flipped = results.tile([P, queries], F32, name="flipped", align_bytes=64)
             nc.vector.transpose(flipped[:], quotient[:])
             for a in range(P // SQUARE):
-                column = first + a * P
+                column = first + a * run
                 nc.sync.dma_start(
-                    out_squares[h][:, :, column : column + P],
-                    flipped[a * SQUARE : (a + 1) * SQUARE, :].rearrange("r (b n) -> r b n", n=P),
+                    out_squares[h][:, :, column : column + run],
+                    flipped[a * SQUARE : (a + 1) * SQUARE, :].rearrange("r (b n) -> r b n", n=run),
                 )
 
         first_pieces = N // PIECE + 1
         for n in range(first_pieces):
             prepare(n)
 
-        steps = [
-            (0, unit, block)
-            for first in range(0, BLOCKS, PIECE // P)
-            for unit in range(UNITS)
-            for block in range(first, first + PIECE // P)
-        ]
-        steps += [(h, unit, block) for h in range(1, HEADS) for unit in range(UNITS) for block in range(BLOCKS)]
-        steps_to_a_piece = UNITS * BLOCKS // (N // PIECE)
+        units = [(h, first, QUERIES) for h in range(HEADS) for first in range(0, M, QUERIES)][:-1]
+        units += [(HEADS - 1, first, QUERIES // 2) for first in range(M - QUERIES, M, QUERIES // 2)]
+
+        both = M // QUERIES
+        steps = [unit + (block,) for unit in units[:both] for block in range(PIECE // P)]
+        steps += [unit + (block,) for unit in units[:both] for block in range(PIECE // P, BLOCKS)]
+        steps += [unit + (block,) for unit in units[both:] for block in range(0, BLOCKS, BANK // unit[2])]
+        steps_to_a_piece = M // QUERIES * BLOCKS // (N // PIECE)
         banks = {}
         sums = {}
         for t in range(-AHEAD, len(steps)):
             if 0 <= t < len(steps):
-                e = exponential(banks[t])
+                h, first, queries, block = steps[t]
+                e = exponential(banks[t], queries)
             if t + AHEAD < len(steps):
-                h, unit, block = steps[t + AHEAD]
-                banks[t + AHEAD] = score(h, unit, block)
+                h, first, queries, block = steps[t + AHEAD]
+                banks[t + AHEAD] = score(h, first, queries, block)
             if 0 <= t < len(steps):
-                h, unit, block = steps[t]
+                h, first, queries, block = steps[t]
                 if block == 0:
-                    sums[unit] = [sum_banks.tile([P, 2, 2 * D], F32, name="sums") for w in range(QUERY_BLOCKS // 2)]
-                accumulate(h, block, e, sums[unit])
-                if block == BLOCKS - 1:
-                    finish(h, unit, sums[unit])
+                    sums[first] = [sum_banks.tile([P, 2, 2 * D], F32, name="sums") for w in range(queries // (2 * P))]
+                accumulate(h, queries, block, e, sums[first])
+                if block + BANK // queries == BLOCKS:
+                    finish(h, first, queries, sums[first])
                 if t % steps_to_a_piece == 0 and first_pieces + t // steps_to_a_piece < len(pieces):
                     prepare(first_pieces + t // steps_to_a_piece)

@@ -7,7 +7,6 @@ BF16 = mybir.dt.bfloat16
 U16 = mybir.dt.uint16
 MULT = mybir.AluOpType.mult
 EXP = mybir.ActivationFunctionType.Exp
-COPY = mybir.ActivationFunctionType.Copy
 
 P = 128
 HEADS = 4
@@ -96,23 +95,17 @@ def tile_sfaanetwork_b_kernel(tc, kt, ksc, q, v, vsc, offs, out):
                 MULT,
             )
 
-        def scale_values_early(h, first, count):
-            for block in range(first // P, (first + count) // P):
-                nc.scalar.activation(
-                    out=vd_one[h][:, block, 0:D], in_=v_sb[h][:, block, :], func=COPY, scale=vsc_sb[:, block, h : h + 1]
-                )
-
         halves = [(0, 0, PIECE // 2), (0, PIECE // 2, PIECE // 2)]
         pieces = halves + [(h, first, PIECE) for h in range(HEADS) for first in range(0, N, PIECE)][1:]
 
         def prepare(n):
             h, first, count = pieces[n]
             kd = look_up(h, first, count)
-            if n < len(halves):
-                scale_values_early(h, first, count)
-            else:
+            if n >= len(halves):
                 scale_values(h, first, count)
             round_keys(h, first, count, kd)
+            if n == len(halves) - 1:
+                scale_values(h, 0, PIECE)
 
         def score(h, first, queries, block):
             scores = score_banks.tile([P, BANK // queries, queries], F32, name="scores")

@@ -50,9 +50,9 @@ def tile_sfaanetwork_b_kernel(tc, kt, ksc, q, v, vsc, offs, out):
             rows = slice(h * D, (h + 1) * D)
             nc.sync.dma_start(kt_sb[h][:], kt[rows, :])
             if h == 0:
-                nc.sync.dma_start(ksc_sb[h][:, 0 : PIECE // 2], ksc[rows, 0 : PIECE // 2])
+                nc.sync.dma_start(ksc_sb[h][:, 0:P], ksc[rows, 0:P])
                 nc.sync.dma_start(q_sb[h][:, 0:QUERIES], q[rows, 0:QUERIES])
-                nc.sync.dma_start(ksc_sb[h][:, PIECE // 2 : PIECE], ksc[rows, PIECE // 2 : PIECE])
+                nc.sync.dma_start(ksc_sb[h][:, P:PIECE], ksc[rows, P:PIECE])
             for first in range(0, N, PIECE):
                 cols = slice(first, first + PIECE)
                 blocks = slice(first // P, (first + PIECE) // P)
@@ -95,16 +95,16 @@ def tile_sfaanetwork_b_kernel(tc, kt, ksc, q, v, vsc, offs, out):
                 MULT,
             )
 
-        halves = [(0, 0, PIECE // 2), (0, PIECE // 2, PIECE // 2)]
-        pieces = halves + [(h, first, PIECE) for h in range(HEADS) for first in range(0, N, PIECE)][1:]
+        parts = [(0, 0, P), (0, P, P), (0, 2 * P, PIECE - 2 * P)]
+        pieces = parts + [(h, first, PIECE) for h in range(HEADS) for first in range(0, N, PIECE)][1:]
 
         def prepare(n):
             h, first, count = pieces[n]
             kd = look_up(h, first, count)
-            if n >= len(halves):
+            if n >= len(parts):
                 scale_values(h, first, count)
             round_keys(h, first, count, kd)
-            if n == len(halves) - 1:
+            if n == len(parts) - 1:
                 scale_values(h, 0, PIECE)
 
         def score(h, first, queries, block):
@@ -132,7 +132,7 @@ def tile_sfaanetwork_b_kernel(tc, kt, ksc, q, v, vsc, offs, out):
                         lhsT=e[:, k, i * P : (i + 1) * P],
                         rhs=vd_one[h][:, block + k, 0 : D + 1],
                         start=(block + k == 0 and i % 2 == 0),
-                        stop=(block + k == BLOCKS - 1 and i % 2 == 1),
+                        stop=(block + k == BLOCKS - 1 and (i % 2 == 1 or queries == P)),
                     )
 
         def finish(h, first, queries, sums):
@@ -140,13 +140,14 @@ def tile_sfaanetwork_b_kernel(tc, kt, ksc, q, v, vsc, offs, out):
             run = query_blocks * SQUARE
             quotient = results.tile([P, queries], F32, name="quotient", align_bytes=64)
             by_query_block = quotient[:].rearrange("p (b i r) -> p i b r", i=query_blocks, r=SQUARE)
-            for w in range(query_blocks // 2):
-                inverse = results.tile([P, 2, 1, 1], F32, name="inverse")
-                nc.vector.reciprocal(inverse[:, :, :, 0], sums[w][:, :, D : D + 1])
+            in_bank = min(2, query_blocks)
+            for w in range(query_blocks // in_bank):
+                inverse = results.tile([P, in_bank, 1, 1], F32, name="inverse")
+                nc.vector.reciprocal(inverse[:, :, :, 0], sums[w][:, 0:in_bank, D : D + 1])
                 nc.vector.tensor_tensor(
-                    by_query_block[:, 2 * w : 2 * w + 2],
-                    sums[w][:, :, 0:D].rearrange("p k (b r) -> p k b r", r=SQUARE),
-                    inverse[:].to_broadcast([P, 2, D // SQUARE, SQUARE]),
+                    by_query_block[:, in_bank * w : in_bank * (w + 1)],
+                    sums[w][:, 0:in_bank, 0:D].rearrange("p k (b r) -> p k b r", r=SQUARE),
+                    inverse[:].to_broadcast([P, in_bank, D // SQUARE, SQUARE]),
                     MULT,
                 )
             flipped = results.tile([P, queries], F32, name="flipped", align_bytes=64)
@@ -158,16 +159,18 @@ def tile_sfaanetwork_b_kernel(tc, kt, ksc, q, v, vsc, offs, out):
                     flipped[a * SQUARE : (a + 1) * SQUARE, :].rearrange("r (b n) -> r b n", n=run),
                 )
 
-        first_pieces = N // PIECE + 1
+        first_pieces = N // PIECE + len(parts) - 1
         for n in range(first_pieces):
             prepare(n)
 
         units = [(h, first, QUERIES) for h in range(HEADS) for first in range(0, M, QUERIES)][:-1]
-        units += [(HEADS - 1, first, QUERIES // 2) for first in range(M - QUERIES, M, QUERIES // 2)]
+        units += [(HEADS - 1, M - QUERIES, QUERIES // 2), (HEADS - 1, M - QUERIES // 2, P), (HEADS - 1, M - P, P)]
 
         both = M // QUERIES
-        steps = [unit + (block,) for unit in units[:both] for block in range(PIECE // P)]
-        steps += [unit + (block,) for unit in units[:both] for block in range(PIECE // P, BLOCKS)]
+        steps = []
+        for first in range(0, BLOCKS // 2, PIECE // P):
+            steps += [unit + (block,) for unit in units[:both] for block in range(first, first + PIECE // P)]
+        steps += [unit + (block,) for unit in units[:both] for block in range(BLOCKS // 2, BLOCKS)]
         steps += [unit + (block,) for unit in units[both:] for block in range(0, BLOCKS, BANK // unit[2])]
         steps_to_a_piece = M // QUERIES * BLOCKS // (N // PIECE)
         banks = {}
@@ -182,7 +185,7 @@ def tile_sfaanetwork_b_kernel(tc, kt, ksc, q, v, vsc, offs, out):
             if 0 <= t < len(steps):
                 h, first, queries, block = steps[t]
                 if block == 0:
-                    sums[first] = [sum_banks.tile([P, 2, 2 * D], F32, name="sums") for w in range(queries // (2 * P))]
+                    sums[first] = [sum_banks.tile([P, 2, 2 * D], F32, name="sums") for w in range(max(1, queries // (2 * P)))]
                 accumulate(h, queries, block, e, sums[first])
                 if block + BANK // queries == BLOCKS:
                     finish(h, first, queries, sums[first])

import math

import concourse.mybir as mybir

F32 = mybir.dt.float32
BF16 = mybir.dt.bfloat16
U16 = mybir.dt.uint16
MULT = mybir.AluOpType.mult
EXP = mybir.ActivationFunctionType.Exp

P = 128
HEADS = 4
D = 128
S = 4096
N = 2048
M = 1024
SCALE = 1.0 / math.sqrt(D)

PIECE = 512
BLOCKS = N // P
BANK = 512
QUERIES = 512
AHEAD = 4
SQUARE = 32
VD_STEP = D + 16

FLOPS = 2 * 2 * HEADS * D * N * M


def tile_sfaanetwork_b_kernel(tc, kt, ksc, q, v, vsc, offs, out):
    nc = tc.nc
    with (
        tc.tile_pool(name="held", bufs=1) as held,
        tc.tile_pool(name="products", bufs=2) as products,
        tc.tile_pool(name="weights", bufs=6) as weights,
        tc.tile_pool(name="results", bufs=2) as results,
        tc.psum_pool(name="score_banks", bufs=AHEAD) as score_banks,
        tc.psum_pool(name="sum_banks", bufs=4) as sum_banks,
    ):
        offsets = held.tile([P, N // 16], U16, name="offsets")
        nc.sync.dma_start(offsets[:], offs)
        vsc_sb = held.tile([P, BLOCKS, 2 * HEADS], F32, name="vsc_sb")
        v_blocks = v.rearrange("(b p) c -> p b c", p=P)
        vsc_blocks = vsc.rearrange("(b p) h -> p b h", p=P)
        kt_sb = [held.tile([P, S], F32, name=f"kt{h}") for h in range(HEADS)]
        ksc_sb = [held.tile([P, N], F32, name=f"ksc{h}") for h in range(HEADS)]
        q_sb = [held.tile([P, M], BF16, name=f"q{h}") for h in range(HEADS)]
        v_sb = [held.tile([P, BLOCKS, D], F32, name=f"v{h}") for h in range(HEADS)]
        for h in range(HEADS):
            rows = slice(h * D, (h + 1) * D)
            nc.sync.dma_start(kt_sb[h][:], kt[rows, :])
            if h == 0:
                nc.sync.dma_start(ksc_sb[h][:, 0:P], ksc[rows, 0:P])
                nc.sync.dma_start(q_sb[h][:, 0:QUERIES], q[rows, 0:QUERIES])
                nc.sync.dma_start(ksc_sb[h][:, P:PIECE], ksc[rows, P:PIECE])
            for first in range(0, N, PIECE):
                cols = slice(first, first + PIECE)
                blocks = slice(first // P, (first + PIECE) // P)
                if h > 0 or first > 0:
                    nc.sync.dma_start(ksc_sb[h][:, cols], ksc[rows, cols])
                if h == 0 and first == 0:
                    nc.sync.dma_start(q_sb[h][:, QUERIES:M], q[rows, QUERIES:M])
                if h == 0:
                    nc.sync.dma_start(vsc_sb[:, blocks, 0:HEADS], vsc_blocks[:, blocks, :])
                nc.sync.dma_start(v_sb[h][:, blocks, :], v_blocks[:, blocks, rows])
                if h > 0 and first == 0:
                    nc.sync.dma_start(q_sb[h][:], q[rows, :])

        out_squares = [out[h * D : (h + 1) * D, :].rearrange("(b r) m -> r b m", r=SQUARE) for h in range(HEADS)]

        kd_bf = [held.tile([P, N], BF16, name=f"kd_bf{h}") for h in range(HEADS)]
        vd_one = [held.tile([P, BLOCKS, VD_STEP], BF16, name=f"vd_one{h}") for h in range(HEADS)]
        for h in range(HEADS):
            nc.gpsimd.memset(vd_one[h][:, :, D : D + 1], 1.0)

        def look_up(h, first, count):
            kd = products.tile([P, count], F32, name="kd")
            nc.vector.tensor_tensor(
                kd[:],
                kt_sb[h][:].indirect(offsets[:, first // 16 : (first + count) // 16]),
                ksc_sb[h][:, first : first + count],
                MULT,
            )
            return kd

        def round_keys(h, first, count, kd):
            nc.vector.tensor_copy(kd_bf[h][:, first : first + count], kd[:])

        def scale_values(h, first, count):
            blocks = slice(first // P, (first + count) // P)
            nc.vector.tensor_tensor(
                vd_one[h][:, blocks, 0:D],
                v_sb[h][:, blocks, :],
                vsc_sb[:, blocks, h : h + 1].to_broadcast([P, count // P, D]),
                MULT,
            )

        parts = [(0, 0, P), (0, P, P), (0, 2 * P, PIECE - 2 * P)]
        pieces = parts + [(h, first, PIECE) for h in range(HEADS) for first in range(0, N, PIECE)][1:]

        def prepare(n):
            h, first, count = pieces[n]
            kd = look_up(h, first, count)
            if n >= len(parts):
                scale_values(h, first, count)
            round_keys(h, first, count, kd)
            if n == len(parts) - 1:
                scale_values(h, 0, PIECE)

        def score(h, first, queries, block):
            scores = score_banks.tile([P, BANK // queries, queries], F32, name="scores")
            for k in range(BANK // queries):
                nc.tensor.matmul(
                    scores[:, k, :].rearrange("p (i a c) -> p a i c", i=queries // P, c=SQUARE),
                    lhsT=kd_bf[h][:, (block + k) * P : (block + k + 1) * P],
                    rhs=q_sb[h][:, first : first + queries],
                    start=True,
                    stop=True,
                )
            return scores

        def exponential(scores, queries):
            e = weights.tile([P, BANK // queries, queries], BF16, name="e")
            nc.scalar.activation(out=e[:], in_=scores[:], func=EXP, scale=SCALE)
            return e

        def accumulate(h, queries, block, e, sums):
            for k in range(BANK // queries):
                for i in range(queries // P):
                    nc.tensor.matmul(
                        sums[i // 2][:, i % 2, 0 : D + 1],
                        lhsT=e[:, k, i * P : (i + 1) * P],
                        rhs=vd_one[h][:, block + k, 0 : D + 1],
                        start=(block + k == 0 and i % 2 == 0),
                        stop=(block + k == BLOCKS - 1 and (i % 2 == 1 or queries == P)),
                    )

        def finish(h, first, queries, sums):
            query_blocks = queries // P
            run = query_blocks * SQUARE
            quotient = results.tile([P, queries], F32, name="quotient", align_bytes=64)
            by_query_block = quotient[:].rearrange("p (b i r) -> p i b r", i=query_blocks, r=SQUARE)
            in_bank = min(2, query_blocks)
            for w in range(query_blocks // in_bank):
                inverse = results.tile([P, in_bank, 1, 1], F32, name="inverse")
                nc.vector.reciprocal(inverse[:, :, :, 0], sums[w][:, 0:in_bank, D : D + 1])
                nc.vector.tensor_tensor(
                    by_query_block[:, in_bank * w : in_bank * (w + 1)],
                    sums[w][:, 0:in_bank, 0:D].rearrange("p k (b r) -> p k b r", r=SQUARE),
                    inverse[:].to_broadcast([P, in_bank, D // SQUARE, SQUARE]),
                    MULT,
                )
            flipped = results.tile([P, queries], F32, name="flipped", align_bytes=64)
            nc.vector.transpose(flipped[:], quotient[:])
            for a in range(P // SQUARE):
                column = first + a * run
                nc.sync.dma_start(
                    out_squares[h][:, :, column : column + run],
                    flipped[a * SQUARE : (a + 1) * SQUARE, :].rearrange("r (b n) -> r b n", n=run),
                )

        first_pieces = N // PIECE + len(parts) - 1
        for n in range(first_pieces):
            prepare(n)

        units = [(h, first, QUERIES) for h in range(HEADS) for first in range(0, M, QUERIES)][:-1]
        units += [(HEADS - 1, M - QUERIES, QUERIES // 2), (HEADS - 1, M - QUERIES // 2, P), (HEADS - 1, M - P, P)]

        both = M // QUERIES
        steps = []
        for first in range(0, BLOCKS // 2, PIECE // P):
            steps += [unit + (block,) for unit in units[:both] for block in range(first, first + PIECE // P)]
        steps += [unit + (block,) for unit in units[:both] for block in range(BLOCKS // 2, BLOCKS)]
        steps += [unit + (block,) for unit in units[both:] for block in range(0, BLOCKS, BANK // unit[2])]
        steps_to_a_piece = M // QUERIES * BLOCKS // (N // PIECE)
        banks = {}
        sums = {}
        for t in range(-AHEAD, len(steps)):
            if 0 <= t < len(steps):
                h, first, queries, block = steps[t]
                e = exponential(banks[t], queries)
            if t + AHEAD < len(steps):
                h, first, queries, block = steps[t + AHEAD]
                banks[t + AHEAD] = score(h, first, queries, block)
            if 0 <= t < len(steps):
                h, first, queries, block = steps[t]
                if block == 0:
                    sums[first] = [sum_banks.tile([P, 2, 2 * D], F32, name="sums") for w in range(max(1, queries // (2 * P)))]
                accumulate(h, queries, block, e, sums[first])
                if block + BANK // queries == BLOCKS:
                    finish(h, first, queries, sums[first])
                if t % steps_to_a_piece == 0 and first_pieces + t // steps_to_a_piece < len(pieces):
                    prepare(first_pieces + t // steps_to_a_piece)
